import numpy as np
import ml_dtypes

BF16 = ml_dtypes.bfloat16


def bf(x):
    return np.asarray(x, np.float32).astype(BF16)


def f32(x):
    return np.asarray(x, np.float32)


def f64(x):
    return np.asarray(x).astype(np.float64)


def striped(idx):
    return np.tile(idx.reshape(-1, 16).T, (8, 1))


C, S, P, A, B, H1, H2, N = 512, 2048, 2, 4, 1024, 1024, 1024, 8192


def setup_inputs():
    idx = np.concatenate([np.random.permutation(S)[:B] for _ in range(P * A)])
    return {"w_ft": f32(np.random.standard_normal((C, S)) / np.sqrt(A)), "b_ft": f32(0.1 * np.random.standard_normal((C, 1))), "w1": bf(np.random.standard_normal((P * C, H1)) * np.sqrt(2.0 / (P * C))), "b1": f32(0.1 * np.random.standard_normal((H1, 1))), "w2": bf(np.random.standard_normal((H1, H2)) * np.sqrt(2.0 / H1)), "b2": f32(0.1 * np.random.standard_normal((H2, 1))), "offs": striped(idx)}


def reference(w_ft, b_ft, w1, b1, w2, b2, offs):
    idx = offs[:16].T.reshape(-1)
    picked = f64(w_ft)[:, idx].reshape(C, P, A, B)
    feat = np.maximum(picked.sum(axis=2) + f64(b_ft)[:, :, None], 0.0)
    h1 = np.maximum(f64(w1)[:C].T @ feat[:, 0] + f64(w1)[C:].T @ feat[:, 1] + f64(b1), 0.0)
    return np.maximum(f64(w2).T @ h1 + f64(b2), 0.0)

@@ -1,0 +1,116 @@
+import concourse.mybir as mybir
+
+F32 = mybir.dt.float32
+BF16 = mybir.dt.bfloat16
+U16 = mybir.dt.uint16
+ADD = mybir.AluOpType.add
+RELU = mybir.ActivationFunctionType.Relu
+
+P = 128
+CHANNELS = 512
+FEATURES = 2048
+POSITIONS = 1024
+PERSPECTIVES = 2
+SLOTS = 4
+HIDDEN = 1024
+
+CBLOCKS = CHANNELS // P
+KBLOCKS = PERSPECTIVES * CBLOCKS
+HBLOCKS = HIDDEN // P
+CHUNK = 256
+NCHUNKS = POSITIONS // CHUNK
+PER_COLUMN = 16
+
+FLOPS = 2 * POSITIONS * (PERSPECTIVES * CHANNELS * HIDDEN + HIDDEN * HIDDEN)
+
+
+def tile_nnueevaluator_b_kernel(tc, w_ft, b_ft, w1, b1, w2, b2, offs, out):
+    nc = tc.nc
+    with (
+        tc.tile_pool(name="held", bufs=1) as held,
+        tc.tile_pool(name="acc_pool", bufs=8) as acc_pool,
+        tc.tile_pool(name="feat_pool", bufs=2) as feat_pool,
+        tc.tile_pool(name="h1_pool", bufs=2) as h1_pool,
+        tc.tile_pool(name="out_pool", bufs=4) as out_pool,
+        tc.psum_pool(name="psum", bufs=8) as psum,
+    ):
+        offsets = held.tile([P, PERSPECTIVES * SLOTS * POSITIONS // PER_COLUMN], U16, name="offsets")
+        nc.sync.dma_start(offsets[:], offs)
+
+        bft_sb = held.tile([P, CBLOCKS], F32, name="bft_sb")
+        b1_sb = held.tile([P, HBLOCKS], F32, name="b1_sb")
+        b2_sb = held.tile([P, HBLOCKS], F32, name="b2_sb")
+        with nc.allow_non_contiguous_dma(reason="a bias vector, one value to a partition"):
+            nc.scalar.dma_start(bft_sb[:], b_ft.rearrange("(a p) o -> p (a o)", p=P))
+            nc.scalar.dma_start(b1_sb[:], b1.rearrange("(a p) o -> p (a o)", p=P))
+            nc.scalar.dma_start(b2_sb[:], b2.rearrange("(a p) o -> p (a o)", p=P))
+
+        table = [held.tile([P, FEATURES], F32, name=f"table{cb}") for cb in range(CBLOCKS)]
+        w1_sb = [held.tile([P, HIDDEN], BF16, name=f"w1_sb{k}") for k in range(KBLOCKS)]
+        w2_sb = [held.tile([P, HIDDEN], BF16, name=f"w2_sb{m}") for m in range(HBLOCKS)]
+        for cb in range(CBLOCKS):
+            nc.sync.dma_start(table[cb][:], w_ft[cb * P : (cb + 1) * P, :])
+            for persp in range(PERSPECTIVES):
+                k = persp * CBLOCKS + cb
+                nc.sync.dma_start(w1_sb[k][:], w1[k * P : (k + 1) * P, :])
+        for m in range(HBLOCKS):
+            nc.sync.dma_start(w2_sb[m][:], w2[m * P : (m + 1) * P, :])
+
+        zeros = held.tile([P, CHUNK], F32, name="zeros")
+        nc.vector.memset(zeros[:], 0.0)
+        bias_wide = [held.tile([P, CHUNK], F32, name=f"bias_wide{cb}") for cb in range(CBLOCKS)]
+        for cb in range(CBLOCKS):
+            nc.vector.tensor_scalar_add(bias_wide[cb][:], zeros[:], bft_sb[:, cb : cb + 1])
+
+        def build_features(chunk, cb, feat):
+            acc = [bias_wide[cb], bias_wide[cb]]
+            for slot in range(SLOTS):
+                for persp in range(PERSPECTIVES):
+                    run = persp * SLOTS + slot
+                    first = (run * POSITIONS + chunk * CHUNK) // PER_COLUMN
+                    picked = table[cb][:].indirect(offsets[:, first : first + CHUNK // PER_COLUMN])
+                    total = acc_pool.tile([P, CHUNK], F32, name=f"acc{persp}")
+                    nc.vector.tensor_tensor(total[:], picked, acc[persp][:], ADD)
+                    acc[persp] = total
+            for persp in range(PERSPECTIVES):
+                k = persp * CBLOCKS + cb
+                feat[k] = feat_pool.tile([P, CHUNK], BF16, name=f"feat{k}")
+                nc.scalar.activation(feat[k][:], acc[persp][:], RELU)
+
+        k_order = [persp * CBLOCKS + cb for cb in range(CBLOCKS) for persp in range(PERSPECTIVES)]
+        k_early, k_late = k_order[:-PERSPECTIVES], k_order[-PERSPECTIVES:]
+
+        for chunk in range(NCHUNKS):
+            feat = {}
+            for cb in range(CBLOCKS):
+                build_features(chunk, cb, feat)
+
+            sums = [psum.tile([P, CHUNK], F32, name=f"sum{m}", tag="bank") for m in range(HBLOCKS)]
+            for k in k_early:
+                for m in range(HBLOCKS):
+                    nc.tensor.matmul(
+                        sums[m][:], w1_sb[k][:, m * P : (m + 1) * P], feat[k][:],
+                        start=(k == k_early[0]), stop=False,
+                    )
+            h1 = []
+            for m in range(HBLOCKS):
+                for k in k_late:
+                    nc.tensor.matmul(
+                        sums[m][:], w1_sb[k][:, m * P : (m + 1) * P], feat[k][:],
+                        start=False, stop=(k == k_late[-1]),
+                    )
+                h1.append(h1_pool.tile([P, CHUNK], BF16, name=f"h1_{m}"))
+                nc.scalar.activation(h1[m][:], sums[m][:], RELU, bias=b1_sb[:, m : m + 1])
+
+            for n in range(HBLOCKS):
+                total = psum.tile([P, CHUNK], F32, name="total", tag="bank")
+                for m in range(HBLOCKS):
+                    nc.tensor.matmul(
+                        total[:], w2_sb[m][:, n * P : (n + 1) * P], h1[m][:],
+                        start=(m == 0), stop=(m == HBLOCKS - 1),
+                    )
+                result = out_pool.tile([P, CHUNK], F32, name="result")
+                nc.scalar.activation(result[:], total[:], RELU, bias=b2_sb[:, n : n + 1])
+                nc.sync.dma_start(
+                    out[n * P : (n + 1) * P, chunk * CHUNK : (chunk + 1) * CHUNK], result[:]
+                )

@@ -31,7 +31,7 @@ def tile_nnueevaluator_b_kernel(tc, w_ft, b_ft, w1, b1, w2, b2, offs, out):
         tc.tile_pool(name="acc_pool", bufs=8) as acc_pool,
         tc.tile_pool(name="feat_pool", bufs=2) as feat_pool,
         tc.tile_pool(name="h1_pool", bufs=2) as h1_pool,
-        tc.tile_pool(name="out_pool", bufs=4) as out_pool,
+        tc.tile_pool(name="out_pool", bufs=8) as out_pool,
         tc.psum_pool(name="psum", bufs=8) as psum,
     ):
         offsets = held.tile([P, PERSPECTIVES * SLOTS * POSITIONS // PER_COLUMN], U16, name="offsets")
@@ -74,7 +74,7 @@ def tile_nnueevaluator_b_kernel(tc, w_ft, b_ft, w1, b1, w2, b2, offs, out):
                     acc[persp] = total
             for persp in range(PERSPECTIVES):
                 k = persp * CBLOCKS + cb
-                feat[k] = feat_pool.tile([P, CHUNK], BF16, name=f"feat{k}")
+                feat[k] = feat_pool.tile([P, CHUNK], BF16, name=f"feat{k}", tag="feat")
                 nc.scalar.activation(feat[k][:], acc[persp][:], RELU)
 
         k_order = [persp * CBLOCKS + cb for cb in range(CBLOCKS) for persp in range(PERSPECTIVES)]

@@ -42,8 +42,6 @@ def tile_nnueevaluator_b_kernel(tc, w_ft, b_ft, w1, b1, w2, b2, offs, out):
         b2_sb = held.tile([P, HBLOCKS], F32, name="b2_sb")
         with nc.allow_non_contiguous_dma(reason="a bias vector, one value to a partition"):
             nc.scalar.dma_start(bft_sb[:], b_ft.rearrange("(a p) o -> p (a o)", p=P))
-            nc.scalar.dma_start(b1_sb[:], b1.rearrange("(a p) o -> p (a o)", p=P))
-            nc.scalar.dma_start(b2_sb[:], b2.rearrange("(a p) o -> p (a o)", p=P))
 
         table = [held.tile([P, FEATURES], F32, name=f"table{cb}") for cb in range(CBLOCKS)]
         w1_sb = [held.tile([P, HIDDEN], BF16, name=f"w1_sb{k}") for k in range(KBLOCKS)]
@@ -53,8 +51,12 @@ def tile_nnueevaluator_b_kernel(tc, w_ft, b_ft, w1, b1, w2, b2, offs, out):
             for persp in range(PERSPECTIVES):
                 k = persp * CBLOCKS + cb
                 nc.sync.dma_start(w1_sb[k][:], w1[k * P : (k + 1) * P, :])
+        with nc.allow_non_contiguous_dma(reason="a bias vector, one value to a partition"):
+            nc.sync.dma_start(b1_sb[:], b1.rearrange("(a p) o -> p (a o)", p=P))
         for m in range(HBLOCKS):
             nc.sync.dma_start(w2_sb[m][:], w2[m * P : (m + 1) * P, :])
+        with nc.allow_non_contiguous_dma(reason="a bias vector, one value to a partition"):
+            nc.sync.dma_start(b2_sb[:], b2.rearrange("(a p) o -> p (a o)", p=P))
 
         zeros = held.tile([P, CHUNK], F32, name="zeros")
         nc.vector.memset(zeros[:], 0.0)

@@ -17,9 +17,10 @@ HIDDEN = 1024
 CBLOCKS = CHANNELS // P
 KBLOCKS = PERSPECTIVES * CBLOCKS
 HBLOCKS = HIDDEN // P
-CHUNK = 256
-NCHUNKS = POSITIONS // CHUNK
 PER_COLUMN = 16
+WIDTHS = (256, 224, 192, 192, 160)
+WIDEST = max(WIDTHS)
+assert sum(WIDTHS) == POSITIONS and all(width % (2 * PER_COLUMN) == 0 for width in WIDTHS)
 
 FLOPS = 2 * POSITIONS * (PERSPECTIVES * CHANNELS * HIDDEN + HIDDEN * HIDDEN)
 
@@ -28,7 +29,8 @@ def tile_nnueevaluator_b_kernel(tc, w_ft, b_ft, w1, b1, w2, b2, offs, out):
     nc = tc.nc
     with (
         tc.tile_pool(name="held", bufs=1) as held,
-        tc.tile_pool(name="acc_pool", bufs=8) as acc_pool,
+        tc.tile_pool(name="partial_pool", bufs=4) as partial_pool,
+        tc.tile_pool(name="sum_pool", bufs=16) as sum_pool,
         tc.tile_pool(name="feat_pool", bufs=2) as feat_pool,
         tc.tile_pool(name="h1_pool", bufs=2) as h1_pool,
         tc.tile_pool(name="out_pool", bufs=8) as out_pool,
@@ -58,36 +60,40 @@ def tile_nnueevaluator_b_kernel(tc, w_ft, b_ft, w1, b1, w2, b2, offs, out):
         with nc.allow_non_contiguous_dma(reason="a bias vector, one value to a partition"):
             nc.sync.dma_start(b2_sb[:], b2.rearrange("(a p) o -> p (a o)", p=P))
 
-        zeros = held.tile([P, CHUNK], F32, name="zeros")
+        zeros = held.tile([P, WIDEST], F32, name="zeros")
         nc.vector.memset(zeros[:], 0.0)
-        bias_wide = [held.tile([P, CHUNK], F32, name=f"bias_wide{cb}") for cb in range(CBLOCKS)]
+        bias_wide = [held.tile([P, WIDEST], F32, name=f"bias_wide{cb}") for cb in range(CBLOCKS)]
         for cb in range(CBLOCKS):
             nc.vector.tensor_scalar_add(bias_wide[cb][:], zeros[:], bft_sb[:, cb : cb + 1])
 
-        def build_features(chunk, cb, feat):
+        def build_features(start, width, cb, feat):
             acc = [bias_wide[cb], bias_wide[cb]]
             for slot in range(SLOTS):
                 for persp in range(PERSPECTIVES):
                     run = persp * SLOTS + slot
-                    first = (run * POSITIONS + chunk * CHUNK) // PER_COLUMN
-                    picked = table[cb][:].indirect(offsets[:, first : first + CHUNK // PER_COLUMN])
-                    total = acc_pool.tile([P, CHUNK], F32, name=f"acc{persp}")
-                    nc.vector.tensor_tensor(total[:], picked, acc[persp][:], ADD)
+                    first = (run * POSITIONS + start) // PER_COLUMN
+                    picked = table[cb][:].indirect(offsets[:, first : first + width // PER_COLUMN])
+                    if slot == SLOTS - 1:
+                        total = sum_pool.tile([P, width], F32, name=f"sum{persp}")
+                    else:
+                        total = partial_pool.tile([P, width], F32, name=f"partial{persp}")
+                    nc.vector.tensor_tensor(total[:], picked, acc[persp][:, :width], ADD)
                     acc[persp] = total
             for persp in range(PERSPECTIVES):
                 k = persp * CBLOCKS + cb
-                feat[k] = feat_pool.tile([P, CHUNK], BF16, name=f"feat{k}", tag="feat")
+                feat[k] = feat_pool.tile([P, width], BF16, name=f"feat{k}", tag="feat")
                 nc.scalar.activation(feat[k][:], acc[persp][:], RELU)
 
         k_order = [persp * CBLOCKS + cb for cb in range(CBLOCKS) for persp in range(PERSPECTIVES)]
         k_early, k_late = k_order[:-PERSPECTIVES], k_order[-PERSPECTIVES:]
 
-        for chunk in range(NCHUNKS):
+        for chunk, width in enumerate(WIDTHS):
+            start = sum(WIDTHS[:chunk])
             feat = {}
             for cb in range(CBLOCKS):
-                build_features(chunk, cb, feat)
+                build_features(start, width, cb, feat)
 
-            sums = [psum.tile([P, CHUNK], F32, name=f"sum{m}", tag="bank") for m in range(HBLOCKS)]
+            sums = [psum.tile([P, width], F32, name=f"units{m}", tag="bank") for m in range(HBLOCKS)]
             for k in k_early:
                 for m in range(HBLOCKS):
                     nc.tensor.matmul(
@@ -101,18 +107,18 @@ def tile_nnueevaluator_b_kernel(tc, w_ft, b_ft, w1, b1, w2, b2, offs, out):
                         sums[m][:], w1_sb[k][:, m * P : (m + 1) * P], feat[k][:],
                         start=False, stop=(k == k_late[-1]),
                     )
-                h1.append(h1_pool.tile([P, CHUNK], BF16, name=f"h1_{m}"))
+                h1.append(h1_pool.tile([P, width], BF16, name=f"h1_{m}"))
                 nc.scalar.activation(h1[m][:], sums[m][:], RELU, bias=b1_sb[:, m : m + 1])
 
             for n in range(HBLOCKS):
-                total = psum.tile([P, CHUNK], F32, name="total", tag="bank")
+                total = psum.tile([P, width], F32, name="total", tag="bank")
                 for m in range(HBLOCKS):
                     nc.tensor.matmul(
                         total[:], w2_sb[m][:, n * P : (n + 1) * P], h1[m][:],
                         start=(m == 0), stop=(m == HBLOCKS - 1),
                     )
-                result = out_pool.tile([P, CHUNK], F32, name="result")
+                result = out_pool.tile([P, width], F32, name="result")
                 nc.scalar.activation(result[:], total[:], RELU, bias=b2_sb[:, n : n + 1])
                 nc.sync.dma_start(
-                    out[n * P : (n + 1) * P, chunk * CHUNK : (chunk + 1) * CHUNK], result[:]
+                    out[n * P : (n + 1) * P, start : start + width], result[:]
                 )

@@ -18,8 +18,9 @@ CBLOCKS = CHANNELS // P
 KBLOCKS = PERSPECTIVES * CBLOCKS
 HBLOCKS = HIDDEN // P
 PER_COLUMN = 16
-WIDTHS = (256, 224, 192, 192, 160)
+WIDTHS = (256, 224, 192, 160, 128, 64)
 WIDEST = max(WIDTHS)
+FEAT_RING = 4
 assert sum(WIDTHS) == POSITIONS and all(width % (2 * PER_COLUMN) == 0 for width in WIDTHS)
 
 FLOPS = 2 * POSITIONS * (PERSPECTIVES * CHANNELS * HIDDEN + HIDDEN * HIDDEN)
@@ -31,7 +32,7 @@ def tile_nnueevaluator_b_kernel(tc, w_ft, b_ft, w1, b1, w2, b2, offs, out):
         tc.tile_pool(name="held", bufs=1) as held,
         tc.tile_pool(name="partial_pool", bufs=4) as partial_pool,
         tc.tile_pool(name="sum_pool", bufs=16) as sum_pool,
-        tc.tile_pool(name="feat_pool", bufs=2) as feat_pool,
+        tc.tile_pool(name="feat_pool", bufs=FEAT_RING) as feat_pool,
         tc.tile_pool(name="h1_pool", bufs=2) as h1_pool,
         tc.tile_pool(name="out_pool", bufs=8) as out_pool,
         tc.psum_pool(name="psum", bufs=8) as psum,
@@ -85,7 +86,8 @@ def tile_nnueevaluator_b_kernel(tc, w_ft, b_ft, w1, b1, w2, b2, offs, out):
                 nc.scalar.activation(feat[k][:], acc[persp][:], RELU)
 
         k_order = [persp * CBLOCKS + cb for cb in range(CBLOCKS) for persp in range(PERSPECTIVES)]
-        k_early, k_late = k_order[:-PERSPECTIVES], k_order[-PERSPECTIVES:]
+        k_held = k_order[-FEAT_RING:]
+        m_last = HBLOCKS - 1
 
         for chunk, width in enumerate(WIDTHS):
             start = sum(WIDTHS[:chunk])
@@ -94,31 +96,35 @@ def tile_nnueevaluator_b_kernel(tc, w_ft, b_ft, w1, b1, w2, b2, offs, out):
                 build_features(start, width, cb, feat)
 
             sums = [psum.tile([P, width], F32, name=f"units{m}", tag="bank") for m in range(HBLOCKS)]
-            for k in k_early:
-                for m in range(HBLOCKS):
-                    nc.tensor.matmul(
-                        sums[m][:], w1_sb[k][:, m * P : (m + 1) * P], feat[k][:],
-                        start=(k == k_early[0]), stop=False,
-                    )
-            h1 = []
-            for m in range(HBLOCKS):
-                for k in k_late:
-                    nc.tensor.matmul(
-                        sums[m][:], w1_sb[k][:, m * P : (m + 1) * P], feat[k][:],
-                        start=False, stop=(k == k_late[-1]),
-                    )
-                h1.append(h1_pool.tile([P, width], BF16, name=f"h1_{m}"))
-                nc.scalar.activation(h1[m][:], sums[m][:], RELU, bias=b1_sb[:, m : m + 1])
+            h1 = [None] * HBLOCKS
 
-            for n in range(HBLOCKS):
-                total = psum.tile([P, width], F32, name="total", tag="bank")
-                for m in range(HBLOCKS):
-                    nc.tensor.matmul(
-                        total[:], w2_sb[m][:, n * P : (n + 1) * P], h1[m][:],
-                        start=(m == 0), stop=(m == HBLOCKS - 1),
-                    )
-                result = out_pool.tile([P, width], F32, name="result")
-                nc.scalar.activation(result[:], total[:], RELU, bias=b2_sb[:, n : n + 1])
-                nc.sync.dma_start(
-                    out[n * P : (n + 1) * P, start : start + width], result[:]
+            def layer1(k, m):
+                nc.tensor.matmul(
+                    sums[m][:], w1_sb[k][:, m * P : (m + 1) * P], feat[k][:],
+                    start=(k == k_order[0]), stop=(k == k_order[-1]),
                 )
+                if k == k_order[-1]:
+                    h1[m] = h1_pool.tile([P, width], BF16, name=f"h1_{m}")
+                    nc.scalar.activation(h1[m][:], sums[m][:], RELU, bias=b1_sb[:, m : m + 1])
+
+            for k in k_order:
+                for m in range(m_last if k in k_held else HBLOCKS):
+                    layer1(k, m)
+            for k in k_held:
+                layer1(k, m_last)
+
+            for n_first in range(0, HBLOCKS, 2):
+                n_pair = (n_first, n_first + 1)
+                totals = {n: psum.tile([P, width], F32, name=f"total{n}", tag="bank") for n in n_pair}
+                for m in range(HBLOCKS):
+                    for n in n_pair:
+                        nc.tensor.matmul(
+                            totals[n][:], w2_sb[m][:, n * P : (n + 1) * P], h1[m][:],
+                            start=(m == 0), stop=(m == HBLOCKS - 1),
+                        )
+                for n in n_pair:
+                    result = out_pool.tile([P, width], F32, name="result")
+                    nc.scalar.activation(result[:], totals[n][:], RELU, bias=b2_sb[:, n : n + 1])
+                    nc.sync.dma_start(
+                        out[n * P : (n + 1) * P, start : start + width], result[:]
+                    )

@@ -18,7 +18,7 @@ CBLOCKS = CHANNELS // P
 KBLOCKS = PERSPECTIVES * CBLOCKS
 HBLOCKS = HIDDEN // P
 PER_COLUMN = 16
-WIDTHS = (256, 224, 192, 160, 128, 64)
+WIDTHS = (288, 256, 192, 160, 128)
 WIDEST = max(WIDTHS)
 FEAT_RING = 4
 assert sum(WIDTHS) == POSITIONS and all(width % (2 * PER_COLUMN) == 0 for width in WIDTHS)
@@ -107,7 +107,10 @@ def tile_nnueevaluator_b_kernel(tc, w_ft, b_ft, w1, b1, w2, b2, offs, out):
                     h1[m] = h1_pool.tile([P, width], BF16, name=f"h1_{m}")
                     nc.scalar.activation(h1[m][:], sums[m][:], RELU, bias=b1_sb[:, m : m + 1])
 
-            for k in k_order:
+            for m in range(HBLOCKS):
+                for k in k_order[:PERSPECTIVES]:
+                    layer1(k, m)
+            for k in k_order[PERSPECTIVES:]:
                 for m in range(m_last if k in k_held else HBLOCKS):
                     layer1(k, m)
             for k in k_held:

@@ -4,6 +4,7 @@ F32 = mybir.dt.float32
 BF16 = mybir.dt.bfloat16
 U16 = mybir.dt.uint16
 ADD = mybir.AluOpType.add
+MAX = mybir.AluOpType.max
 RELU = mybir.ActivationFunctionType.Relu
 
 P = 128
@@ -85,12 +86,19 @@ def tile_nnueevaluator_b_kernel(tc, w_ft, b_ft, w1, b1, w2, b2, offs, out):
                 feat[k] = feat_pool.tile([P, width], BF16, name=f"feat{k}", tag="feat")
                 nc.scalar.activation(feat[k][:], acc[persp][:], RELU)
 
+        def rectify(block, is_last_chunk, result, bank, bias_column):
+            if is_last_chunk and block % 2 == 1:
+                nc.vector.tensor_scalar(result[:], bank[:], bias_column, 0.0, ADD, MAX)
+            else:
+                nc.scalar.activation(result[:], bank[:], RELU, bias=bias_column)
+
         k_order = [persp * CBLOCKS + cb for cb in range(CBLOCKS) for persp in range(PERSPECTIVES)]
         k_held = k_order[-FEAT_RING:]
         m_last = HBLOCKS - 1
 
         for chunk, width in enumerate(WIDTHS):
             start = sum(WIDTHS[:chunk])
+            is_last_chunk = chunk == len(WIDTHS) - 1
             feat = {}
             for cb in range(CBLOCKS):
                 build_features(start, width, cb, feat)
@@ -105,7 +113,7 @@ def tile_nnueevaluator_b_kernel(tc, w_ft, b_ft, w1, b1, w2, b2, offs, out):
                 )
                 if k == k_order[-1]:
                     h1[m] = h1_pool.tile([P, width], BF16, name=f"h1_{m}")
-                    nc.scalar.activation(h1[m][:], sums[m][:], RELU, bias=b1_sb[:, m : m + 1])
+                    rectify(m, is_last_chunk, h1[m], sums[m], b1_sb[:, m : m + 1])
 
             for m in range(HBLOCKS):
                 for k in k_order[:PERSPECTIVES]:
@@ -127,7 +135,7 @@ def tile_nnueevaluator_b_kernel(tc, w_ft, b_ft, w1, b1, w2, b2, offs, out):
                         )
                 for n in n_pair:
                     result = out_pool.tile([P, width], F32, name="result")
-                    nc.scalar.activation(result[:], totals[n][:], RELU, bias=b2_sb[:, n : n + 1])
+                    rectify(n, is_last_chunk, result, totals[n], b2_sb[:, n : n + 1])
                     nc.sync.dma_start(
                         out[n * P : (n + 1) * P, start : start + width], result[:]
                     )

import concourse.mybir as mybir

F32 = mybir.dt.float32
BF16 = mybir.dt.bfloat16
U16 = mybir.dt.uint16
ADD = mybir.AluOpType.add
MAX = mybir.AluOpType.max
RELU = mybir.ActivationFunctionType.Relu

P = 128
CHANNELS = 512
FEATURES = 2048
POSITIONS = 1024
PERSPECTIVES = 2
SLOTS = 4
HIDDEN = 1024

CBLOCKS = CHANNELS // P
KBLOCKS = PERSPECTIVES * CBLOCKS
HBLOCKS = HIDDEN // P
PER_COLUMN = 16
WIDTHS = (288, 256, 192, 160, 128)
WIDEST = max(WIDTHS)
FEAT_RING = 4
assert sum(WIDTHS) == POSITIONS and all(width % (2 * PER_COLUMN) == 0 for width in WIDTHS)

FLOPS = 2 * POSITIONS * (PERSPECTIVES * CHANNELS * HIDDEN + HIDDEN * HIDDEN)


def tile_nnueevaluator_b_kernel(tc, w_ft, b_ft, w1, b1, w2, b2, offs, out):
    nc = tc.nc
    with (
        tc.tile_pool(name="held", bufs=1) as held,
        tc.tile_pool(name="partial_pool", bufs=4) as partial_pool,
        tc.tile_pool(name="sum_pool", bufs=16) as sum_pool,
        tc.tile_pool(name="feat_pool", bufs=FEAT_RING) as feat_pool,
        tc.tile_pool(name="h1_pool", bufs=2) as h1_pool,
        tc.tile_pool(name="out_pool", bufs=8) as out_pool,
        tc.psum_pool(name="psum", bufs=8) as psum,
    ):
        offsets = held.tile([P, PERSPECTIVES * SLOTS * POSITIONS // PER_COLUMN], U16, name="offsets")
        nc.sync.dma_start(offsets[:], offs)

        bft_sb = held.tile([P, CBLOCKS], F32, name="bft_sb")
        b1_sb = held.tile([P, HBLOCKS], F32, name="b1_sb")
        b2_sb = held.tile([P, HBLOCKS], F32, name="b2_sb")
        with nc.allow_non_contiguous_dma(reason="a bias vector, one value to a partition"):
            nc.scalar.dma_start(bft_sb[:], b_ft.rearrange("(a p) o -> p (a o)", p=P))

        table = [held.tile([P, FEATURES], F32, name=f"table{cb}") for cb in range(CBLOCKS)]
        w1_sb = [held.tile([P, HIDDEN], BF16, name=f"w1_sb{k}") for k in range(KBLOCKS)]
        w2_sb = [held.tile([P, HIDDEN], BF16, name=f"w2_sb{m}") for m in range(HBLOCKS)]
        for cb in range(CBLOCKS):
            nc.sync.dma_start(table[cb][:], w_ft[cb * P : (cb + 1) * P, :])
            for persp in range(PERSPECTIVES):
                k = persp * CBLOCKS + cb
                nc.sync.dma_start(w1_sb[k][:], w1[k * P : (k + 1) * P, :])
        with nc.allow_non_contiguous_dma(reason="a bias vector, one value to a partition"):
            nc.sync.dma_start(b1_sb[:], b1.rearrange("(a p) o -> p (a o)", p=P))
        for m in range(HBLOCKS):
            nc.sync.dma_start(w2_sb[m][:], w2[m * P : (m + 1) * P, :])
        with nc.allow_non_contiguous_dma(reason="a bias vector, one value to a partition"):
            nc.sync.dma_start(b2_sb[:], b2.rearrange("(a p) o -> p (a o)", p=P))

        zeros = held.tile([P, WIDEST], F32, name="zeros")
        nc.vector.memset(zeros[:], 0.0)
        bias_wide = [held.tile([P, WIDEST], F32, name=f"bias_wide{cb}") for cb in range(CBLOCKS)]
        for cb in range(CBLOCKS):
            nc.vector.tensor_scalar_add(bias_wide[cb][:], zeros[:], bft_sb[:, cb : cb + 1])

        def build_features(start, width, cb, feat):
            acc = [bias_wide[cb], bias_wide[cb]]
            for slot in range(SLOTS):
                for persp in range(PERSPECTIVES):
                    run = persp * SLOTS + slot
                    first = (run * POSITIONS + start) // PER_COLUMN
                    picked = table[cb][:].indirect(offsets[:, first : first + width // PER_COLUMN])
                    if slot == SLOTS - 1:
                        total = sum_pool.tile([P, width], F32, name=f"sum{persp}")
                    else:
                        total = partial_pool.tile([P, width], F32, name=f"partial{persp}")
                    nc.vector.tensor_tensor(total[:], picked, acc[persp][:, :width], ADD)
                    acc[persp] = total
            for persp in range(PERSPECTIVES):
                k = persp * CBLOCKS + cb
                feat[k] = feat_pool.tile([P, width], BF16, name=f"feat{k}", tag="feat")
                nc.scalar.activation(feat[k][:], acc[persp][:], RELU)

        def rectify(block, is_last_chunk, result, bank, bias_column):
            if is_last_chunk and block % 2 == 1:
                nc.vector.tensor_scalar(result[:], bank[:], bias_column, 0.0, ADD, MAX)
            else:
                nc.scalar.activation(result[:], bank[:], RELU, bias=bias_column)

        k_order = [persp * CBLOCKS + cb for cb in range(CBLOCKS) for persp in range(PERSPECTIVES)]
        k_held = k_order[-FEAT_RING:]
        m_last = HBLOCKS - 1

        for chunk, width in enumerate(WIDTHS):
            start = sum(WIDTHS[:chunk])
            is_last_chunk = chunk == len(WIDTHS) - 1
            feat = {}
            for cb in range(CBLOCKS):
                build_features(start, width, cb, feat)

            sums = [psum.tile([P, width], F32, name=f"units{m}", tag="bank") for m in range(HBLOCKS)]
            h1 = [None] * HBLOCKS

            def layer1(k, m):
                nc.tensor.matmul(
                    sums[m][:], w1_sb[k][:, m * P : (m + 1) * P], feat[k][:],
                    start=(k == k_order[0]), stop=(k == k_order[-1]),
                )
                if k == k_order[-1]:
                    h1[m] = h1_pool.tile([P, width], BF16, name=f"h1_{m}")
                    rectify(m, is_last_chunk, h1[m], sums[m], b1_sb[:, m : m + 1])

            for m in range(HBLOCKS):
                for k in k_order[:PERSPECTIVES]:
                    layer1(k, m)
            for k in k_order[PERSPECTIVES:]:
                for m in range(m_last if k in k_held else HBLOCKS):
                    layer1(k, m)
            for k in k_held:
                layer1(k, m_last)

            for n_first in range(0, HBLOCKS, 2):
                n_pair = (n_first, n_first + 1)
                totals = {n: psum.tile([P, width], F32, name=f"total{n}", tag="bank") for n in n_pair}
                for m in range(HBLOCKS):
                    for n in n_pair:
                        nc.tensor.matmul(
                            totals[n][:], w2_sb[m][:, n * P : (n + 1) * P], h1[m][:],
                            start=(m == 0), stop=(m == HBLOCKS - 1),
                        )
                for n in n_pair:
                    result = out_pool.tile([P, width], F32, name="result")
                    rectify(n, is_last_chunk, result, totals[n], b2_sb[:, n : n + 1])
                    nc.sync.dma_start(
                        out[n * P : (n + 1) * P, start : start + width], result[:]
                    )
